import numpy as np
import ml_dtypes


def mxq(x, axis, fmt="e4m3"):
    dtype, down = {"e4m3": (ml_dtypes.float8_e4m3fn, 7), "e5m2": (ml_dtypes.float8_e5m2, 14)}[fmt]
    v = np.moveaxis(np.asarray(x, np.float32).astype(ml_dtypes.bfloat16).astype(np.float64), axis, -1)
    blocks = v.reshape(v.shape[:-1] + (-1, 32))
    amax = np.abs(blocks).max(-1, keepdims=True)
    byte = np.maximum(np.where(amax > 0, np.frexp(amax)[1] - 1 + 127, 0) - down, 1)
    scale = np.exp2(byte - 127.0)
    codes = (blocks / scale).astype(np.float32).astype(dtype).astype(np.float64)
    return np.moveaxis((codes * scale).reshape(v.shape), -1, axis)


WIDE = False


def mx_kscale(k):
    if not WIDE:
        return np.ones(k)
    levels = np.array([10, -10, 5, -5, 0])
    a = np.random.permutation(np.resize(levels, k // 512 * 4)).reshape(k // 512, 4)
    idx = np.arange(k)
    return np.exp2(a[idx // 512, idx % 128 // 32])


BF16 = ml_dtypes.bfloat16


def bf(x):
    return np.asarray(x, np.float32).astype(BF16)


def f64(x):
    return np.asarray(x).astype(np.float64)


M, K, N = 1024, 1024, 4096
BLOCK = 128


def setup_inputs():
    s = mx_kscale(K)
    return {"x": bf(np.random.standard_normal((M, K)) * s),
            "weight": bf(np.random.standard_normal((N, K)) / np.sqrt(K) / s[None, :]),
            "weight_scale_inv": bf(np.random.uniform(0.5, 1.5, (N // BLOCK, K // BLOCK))),
            "bias": bf(np.random.standard_normal(N) * 0.3)}


def reference(x, weight, weight_scale_inv, bias):
    n, k = weight.shape
    nb, kb = weight_scale_inv.shape
    w_deq = (f64(weight).reshape(nb, BLOCK, kb, BLOCK) * f64(weight_scale_inv)[:, None, :, None]).reshape(n, k)
    out = mxq(f64(x), 1, "e4m3") @ mxq(w_deq, 1, "e4m3").T
    return out + f64(bias)[None, :]

@@ -1,0 +1,211 @@
+from contextlib import ExitStack
+
+import concourse.mybir as mybir
+from concourse.masks import make_identity
+
+F32 = mybir.dt.float32
+BF16 = mybir.dt.bfloat16
+U32 = mybir.dt.uint32
+U8 = mybir.dt.uint8
+FP8X4 = mybir.dt.float8_e4m3fn_x4
+COPY = mybir.ActivationFunctionType.Copy
+ADD = mybir.AluOpType.add
+
+P = 128
+M, K, N = 1024, 1024, 4096
+FLOPS = 2 * M * K * N
+G = K // 512
+NCH = N // 512
+TB = M // P
+NPIECE = TB // 2
+
+
+def tile_fp8columnparallellinear_kernel(tc, x, weight, weight_scale_inv, bias, out):
+    nc = tc.nc
+    with ExitStack() as ctx:
+        const = ctx.enter_context(tc.tile_pool(name="const", bufs=1))
+        gwp = ctx.enter_context(tc.tile_pool(name="gwp", bufs=2))
+        wqp = ctx.enter_context(tc.tile_pool(name="wqp", bufs=3))
+        stp = ctx.enter_context(tc.tile_pool(name="stp", bufs=6))
+        psum = ctx.enter_context(tc.psum_pool(name="psum", bufs=4))
+        ctx.enter_context(tc.manual_schedule())
+
+        x_view = x.rearrange("(p t) k -> p t k", t=TB)
+        w_view = weight.rearrange("(j p) k -> p j k", p=P)
+        o_view = out.rearrange("(p t) n -> p t n", t=TB)
+
+        ident = const.tile([P, P], F32, name="ident")
+        make_identity(nc, ident[:])
+        s_all = const.tile([P, 256], BF16, name="s_all")
+        nc.scalar.dma_start(
+            out=s_all[:], in_=weight_scale_inv.rearrange("a b -> (a b)").partition_broadcast(P)
+        )
+
+        w_sb = [const.tile([P, 4, K], BF16, name="w_sb%d" % c) for c in range(NCH)]
+        x_sb = [const.tile([P, 2, K], BF16, name="x_sb%d" % i) for i in range(NPIECE)]
+        bias_a = const.tile([P, 1024], BF16, name="bias_a")
+        bias_b = const.tile([P, N - 1024], BF16, name="bias_b")
+
+        def load_w(c):
+            nc.sync.dma_start(out=w_sb[c][:], in_=w_view[:, 4 * c : 4 * c + 4, :])
+
+        for pr in range(2):
+            nc.sync.dma_start(out=w_sb[0][:, 2 * pr : 2 * pr + 2, :], in_=w_view[:, 2 * pr : 2 * pr + 2, :])
+        for i in range(NPIECE):
+            nc.sync.dma_start(out=x_sb[i][:], in_=x_view[:, 2 * i : 2 * i + 2, :])
+        load_w(1)
+        nc.sync.dma_start(out=bias_a[:], in_=bias[0:1024].partition_broadcast(P))
+        load_w(2)
+        nc.sync.dma_start(out=bias_b[:], in_=bias[1024:N].partition_broadcast(P))
+        load_w(3)
+
+        s_nat = const.tile([P, 64], F32, name="s_nat")
+        for q in range(4):
+            nc.vector.tensor_copy(
+                out=s_nat[32 * q : 32 * q + 32, :].rearrange("p (j g) -> p j g", g=2),
+                in_=s_all[32 * q : 32 * q + 32, :].rearrange("p (j g q) -> p j g q", g=2, q=4)[:, :, :, q],
+            )
+
+        xq = [const.tile([P, 512], U32, name="xq%d" % i, align_bytes=64) for i in range(NPIECE)]
+        xs = [const.tile([P, 512], U8, name="xs%d" % i, align_bytes=64) for i in range(NPIECE)]
+        gx = [const.tile([P, 2, 2, P, 4], BF16, name="gx%d" % i, align_bytes=64) for i in range(NPIECE)]
+        gw = {}
+        wq = {}
+        ws = {}
+        wbank = {}
+        xbank = {}
+
+        def words(tile_ap):
+            return tile_ap.bitcast(F32).rearrange("p j (g w u) -> p j g u w", g=G, u=2)
+
+        def t_w(c, order):
+            src = words(w_sb[c][:])
+            for g, pr in order:
+                tp = psum.tile([P, 512], F32, name="tp", tag="tp")
+                for h in range(2):
+                    for u in range(2):
+                        s = 2 * h + u
+                        nc.tensor.transpose(tp[:, s * P : (s + 1) * P], src[:, 2 * pr + h, g, u, :], ident[:])
+                wbank[(c, g, pr)] = tp
+
+        def e_w(c, order):
+            gwc = gwp.tile([P, G, 4, P, 4], BF16, name="gw", tag="gw", align_bytes=64)
+            gw[c] = gwc
+            for g, pr in order:
+                view = wbank[(c, g, pr)][:].bitcast(BF16)
+                for h in range(2):
+                    j = 2 * pr + h
+                    col = (4 * c + j) * 2 + g
+                    nc.scalar.activation(
+                        out=gwc[:, g, j, :, :].rearrange("p r (u e) -> p r u e", e=2),
+                        in_=view[:, h * 512 : (h + 1) * 512].rearrange("p (u r e) -> p r u e", u=2, e=2),
+                        func=COPY,
+                        scale=s_nat[:, col : col + 1],
+                    )
+
+        def q_w(c, g):
+            if g == 0:
+                wqc = wqp.tile([P, G, 512], U32, name="wq", tag="wq", align_bytes=64)
+                wsc = wqp.tile([P, G, 512], U8, name="ws", tag="ws", align_bytes=64)
+                wq[c] = wqc
+                ws[c] = wsc
+            nc.vector.quantize_mx(
+                out=wq[c][:, g, :].bitcast(FP8X4),
+                scales=ws[c][:, g, :],
+                in_=gw[c][:, g, :, :, :].rearrange("p j r t -> p (j r t)"),
+            )
+
+        def t_x(i):
+            src = words(x_sb[i][:])
+            for t2 in range(2):
+                tx = psum.tile([P, 512], F32, name="tx", tag="acc")
+                for g in range(G):
+                    for u in range(2):
+                        s = 2 * g + u
+                        nc.tensor.transpose(tx[:, s * P : (s + 1) * P], src[:, t2, g, u, :], ident[:])
+                xbank[(i, t2)] = tx
+
+        def e_x(i, engine):
+            dst = gx[i][:].bitcast(F32)
+            for t2 in range(2):
+                src = xbank[(i, t2)][:].rearrange("p (g u r) -> p g r u", g=G, u=2)
+                if engine == "v":
+                    nc.vector.tensor_copy(out=dst[:, :, t2, :, :], in_=src)
+                else:
+                    nc.scalar.copy(out=dst[:, :, t2, :, :], in_=src)
+
+        def q_x(i):
+            nc.vector.quantize_mx(
+                out=xq[i][:].bitcast(FP8X4),
+                scales=xs[i][:],
+                in_=gx[i][:].rearrange("p g t r v -> p (g t r v)"),
+            )
+
+        acc = {}
+        stage = {}
+
+        def mx(c, t):
+            i, t2 = t // 2, t % 2
+            a = psum.tile([P, 512], F32, name="acc", tag="acc")
+            acc[(c, t)] = a
+            for g in range(G):
+                cols = slice(g * 256 + t2 * P, g * 256 + t2 * P + P)
+                nc.tensor.matmul_mx(
+                    out=a[:],
+                    lhsT=xq[i][:, cols].bitcast(FP8X4),
+                    lhsT_scale=xs[i][:, cols],
+                    rhs=wq[c][:, g, :].bitcast(FP8X4),
+                    rhs_scale=ws[c][:, g, :],
+                    start=(g == 0),
+                    stop=(g == G - 1),
+                )
+
+        def o(c, t):
+            i, t2 = t // 2, t % 2
+            if t2 == 0:
+                st = stp.tile([P, 2, 512], F32, name="st", tag="st")
+                stage[(c, i)] = st
+            if c < 2:
+                b = bias_a[:, c * 512 : (c + 1) * 512]
+            else:
+                b = bias_b[:, (c - 2) * 512 : (c - 1) * 512]
+            nc.vector.tensor_tensor(out=stage[(c, i)][:, t2, :], in0=acc[(c, t)][:], in1=b, op=ADD)
+            if t2 == 1:
+                nc.sync.dma_start(
+                    out=o_view[:, 2 * i : 2 * i + 2, c * 512 : (c + 1) * 512], in_=stage[(c, i)][:]
+                )
+
+        pair_major = [(0, 0), (1, 0), (0, 1), (1, 1)]
+        pass_major = [(0, 0), (0, 1), (1, 0), (1, 1)]
+
+        t_w(0, pair_major)
+        e_w(0, pair_major)
+        t_x(0)
+        t_x(1)
+        e_x(0, "v")
+        e_x(1, "v")
+        t_x(2)
+        t_x(3)
+        e_x(2, "s")
+        e_x(3, "s")
+        q_w(0, 0)
+        q_x(0)
+        q_w(0, 1)
+        q_x(1)
+        q_x(2)
+        q_x(3)
+
+        for c in range(NCH):
+            if c + 1 < NCH:
+                t_w(c + 1, pass_major)
+                e_w(c + 1, pass_major)
+            for t in range(TB):
+                mx(c, t)
+                o(c, t)
+                if t == 3:
+                    if c + 1 < NCH:
+                        q_w(c + 1, 0)
+                    if c + 4 < NCH:
+                        load_w(c + 4)
+            if c + 1 < NCH:
+                q_w(c + 1, 1)

@@ -25,7 +25,6 @@ def tile_fp8columnparallellinear_kernel(tc, x, weight, weight_scale_inv, bias, o
     with ExitStack() as ctx:
         const = ctx.enter_context(tc.tile_pool(name="const", bufs=1))
         gwp = ctx.enter_context(tc.tile_pool(name="gwp", bufs=2))
-        wqp = ctx.enter_context(tc.tile_pool(name="wqp", bufs=3))
         stp = ctx.enter_context(tc.tile_pool(name="stp", bufs=6))
         psum = ctx.enter_context(tc.psum_pool(name="psum", bufs=4))
         ctx.enter_context(tc.manual_schedule())
@@ -34,17 +33,21 @@ def tile_fp8columnparallellinear_kernel(tc, x, weight, weight_scale_inv, bias, o
         w_view = weight.rearrange("(j p) k -> p j k", p=P)
         o_view = out.rearrange("(p t) n -> p t n", t=TB)
 
-        ident = const.tile([P, P], F32, name="ident")
-        make_identity(nc, ident[:])
+        b_rows = const.tile([P, 512], BF16, name="b_rows")
+        nc.vector.memset(b_rows[:], 0.0)
+        nc.scalar.dma_start(out=b_rows[0:NCH, :], in_=bias.rearrange("(c n) -> c n", c=NCH))
         s_all = const.tile([P, 256], BF16, name="s_all")
         nc.scalar.dma_start(
             out=s_all[:], in_=weight_scale_inv.rearrange("a b -> (a b)").partition_broadcast(P)
         )
+        ident_bf = const.tile([P, P], BF16, name="ident_bf")
+        make_identity(nc, ident_bf[:])
+        ident = const.tile([P, P], F32, name="ident")
+        make_identity(nc, ident[:])
 
         w_sb = [const.tile([P, 4, K], BF16, name="w_sb%d" % c) for c in range(NCH)]
         x_sb = [const.tile([P, 2, K], BF16, name="x_sb%d" % i) for i in range(NPIECE)]
-        bias_a = const.tile([P, 1024], BF16, name="bias_a")
-        bias_b = const.tile([P, N - 1024], BF16, name="bias_b")
+        bias_bc = [const.tile([P, 1024], BF16, name="bias_bc%d" % q) for q in range(4)]
 
         def load_w(c):
             nc.sync.dma_start(out=w_sb[c][:], in_=w_view[:, 4 * c : 4 * c + 4, :])
@@ -54,9 +57,7 @@ def tile_fp8columnparallellinear_kernel(tc, x, weight, weight_scale_inv, bias, o
         for i in range(NPIECE):
             nc.sync.dma_start(out=x_sb[i][:], in_=x_view[:, 2 * i : 2 * i + 2, :])
         load_w(1)
-        nc.sync.dma_start(out=bias_a[:], in_=bias[0:1024].partition_broadcast(P))
         load_w(2)
-        nc.sync.dma_start(out=bias_b[:], in_=bias[1024:N].partition_broadcast(P))
         load_w(3)
 
         s_nat = const.tile([P, 64], F32, name="s_nat")
@@ -69,9 +70,9 @@ def tile_fp8columnparallellinear_kernel(tc, x, weight, weight_scale_inv, bias, o
         xq = [const.tile([P, 512], U32, name="xq%d" % i, align_bytes=64) for i in range(NPIECE)]
         xs = [const.tile([P, 512], U8, name="xs%d" % i, align_bytes=64) for i in range(NPIECE)]
         gx = [const.tile([P, 2, 2, P, 4], BF16, name="gx%d" % i, align_bytes=64) for i in range(NPIECE)]
+        wq = [const.tile([P, G, 512], U32, name="wq%d" % c, align_bytes=64) for c in range(NCH)]
+        ws = [const.tile([P, G, 512], U8, name="ws%d" % c, align_bytes=64) for c in range(NCH)]
         gw = {}
-        wq = {}
-        ws = {}
         wbank = {}
         xbank = {}
 
@@ -104,11 +105,6 @@ def tile_fp8columnparallellinear_kernel(tc, x, weight, weight_scale_inv, bias, o
                     )
 
         def q_w(c, g):
-            if g == 0:
-                wqc = wqp.tile([P, G, 512], U32, name="wq", tag="wq", align_bytes=64)
-                wsc = wqp.tile([P, G, 512], U8, name="ws", tag="ws", align_bytes=64)
-                wq[c] = wqc
-                ws[c] = wsc
             nc.vector.quantize_mx(
                 out=wq[c][:, g, :].bitcast(FP8X4),
                 scales=ws[c][:, g, :],
@@ -141,6 +137,19 @@ def tile_fp8columnparallellinear_kernel(tc, x, weight, weight_scale_inv, bias, o
                 in_=gx[i][:].rearrange("p g t r v -> p (g t r v)"),
             )
 
+        def b_cast(q):
+            pb = psum.tile([P, 1024], BF16, name="pb", tag="acc")
+            for h in range(2):
+                c = 2 * q + h
+                nc.tensor.matmul(
+                    out=pb[:, h * 512 : (h + 1) * 512],
+                    lhsT=ident_bf[:, c : c + 1].to_broadcast([P, P]),
+                    rhs=b_rows[:],
+                    start=True,
+                    stop=True,
+                )
+            nc.scalar.copy(out=bias_bc[q][:], in_=pb[:])
+
         acc = {}
         stage = {}
 
@@ -165,19 +174,18 @@ def tile_fp8columnparallellinear_kernel(tc, x, weight, weight_scale_inv, bias, o
             if t2 == 0:
                 st = stp.tile([P, 2, 512], F32, name="st", tag="st")
                 stage[(c, i)] = st
-            if c < 2:
-                b = bias_a[:, c * 512 : (c + 1) * 512]
-            else:
-                b = bias_b[:, (c - 2) * 512 : (c - 1) * 512]
+            b = bias_bc[c // 2][:, (c % 2) * 512 : (c % 2) * 512 + 512]
             nc.vector.tensor_tensor(out=stage[(c, i)][:, t2, :], in0=acc[(c, t)][:], in1=b, op=ADD)
-            if t2 == 1:
-                nc.sync.dma_start(
-                    out=o_view[:, 2 * i : 2 * i + 2, c * 512 : (c + 1) * 512], in_=stage[(c, i)][:]
-                )
+            cols = slice(c * 512, (c + 1) * 512)
+            if c == NCH - 1 and i == NPIECE - 1:
+                nc.sync.dma_start(out=o_view[:, t, cols], in_=stage[(c, i)][:, t2, :])
+            elif t2 == 1:
+                nc.sync.dma_start(out=o_view[:, 2 * i : 2 * i + 2, cols], in_=stage[(c, i)][:])
 
         pair_major = [(0, 0), (1, 0), (0, 1), (1, 1)]
         pass_major = [(0, 0), (0, 1), (1, 0), (1, 1)]
 
+        b_cast(0)
         t_w(0, pair_major)
         e_w(0, pair_major)
         t_x(0)
@@ -194,18 +202,24 @@ def tile_fp8columnparallellinear_kernel(tc, x, weight, weight_scale_inv, bias, o
         q_x(1)
         q_x(2)
         q_x(3)
+        t_w(1, pass_major)
+        e_w(1, pass_major)
 
-        for c in range(NCH):
-            if c + 1 < NCH:
-                t_w(c + 1, pass_major)
-                e_w(c + 1, pass_major)
-            for t in range(TB):
-                mx(c, t)
-                o(c, t)
-                if t == 3:
-                    if c + 1 < NCH:
-                        q_w(c + 1, 0)
-                    if c + 4 < NCH:
-                        load_w(c + 4)
-            if c + 1 < NCH:
-                q_w(c + 1, 1)
+        RUN = 6
+        for tau in range(NCH * TB):
+            c, t = tau // TB, tau % TB
+            if tau > 0 and tau % RUN == 0 and tau // RUN + 1 < NCH:
+                if tau // RUN < 4:
+                    b_cast(tau // RUN)
+                t_w(tau // RUN + 1, pass_major)
+                e_w(tau // RUN + 1, pass_major)
+            mx(c, t)
+            o(c, t)
+            for cn in range(1, NCH):
+                base = RUN * (cn - 1)
+                if tau == base + 3:
+                    q_w(cn, 0)
+                if tau == base + (5 if cn == 1 else 6):
+                    q_w(cn, 1)
+            if tau % RUN == 1 and tau // RUN + 4 < NCH:
+                load_w(tau // RUN + 4)

@@ -18,6 +18,7 @@ G = K // 512
 NCH = N // 512
 TB = M // P
 NPIECE = TB // 2
+ASSIST = (47, 50, 53, 56, 59)
 
 
 def tile_fp8columnparallellinear_kernel(tc, x, weight, weight_scale_inv, bias, out):
@@ -35,7 +36,6 @@ def tile_fp8columnparallellinear_kernel(tc, x, weight, weight_scale_inv, bias, o
 
         b_rows = const.tile([P, 512], BF16, name="b_rows")
         nc.vector.memset(b_rows[:], 0.0)
-        nc.scalar.dma_start(out=b_rows[0:NCH, :], in_=bias.rearrange("(c n) -> c n", c=NCH))
         s_all = const.tile([P, 256], BF16, name="s_all")
         nc.scalar.dma_start(
             out=s_all[:], in_=weight_scale_inv.rearrange("a b -> (a b)").partition_broadcast(P)
@@ -52,8 +52,10 @@ def tile_fp8columnparallellinear_kernel(tc, x, weight, weight_scale_inv, bias, o
         def load_w(c):
             nc.sync.dma_start(out=w_sb[c][:], in_=w_view[:, 4 * c : 4 * c + 4, :])
 
-        for pr in range(2):
-            nc.sync.dma_start(out=w_sb[0][:, 2 * pr : 2 * pr + 2, :], in_=w_view[:, 2 * pr : 2 * pr + 2, :])
+        for j in range(4):
+            nc.sync.dma_start(out=w_sb[0][:, j, :], in_=w_view[:, j, :])
+            if j == 0:
+                nc.sync.dma_start(out=b_rows[0:NCH, :], in_=bias.rearrange("(c n) -> c n", c=NCH))
         for i in range(NPIECE):
             nc.sync.dma_start(out=x_sb[i][:], in_=x_view[:, 2 * i : 2 * i + 2, :])
         load_w(1)
@@ -79,23 +81,26 @@ def tile_fp8columnparallellinear_kernel(tc, x, weight, weight_scale_inv, bias, o
         def words(tile_ap):
             return tile_ap.bitcast(F32).rearrange("p j (g w u) -> p j g u w", g=G, u=2)
 
-        def t_w(c, order):
+        def t_w(c, banks):
             src = words(w_sb[c][:])
-            for g, pr in order:
+            for units in banks:
                 tp = psum.tile([P, 512], F32, name="tp", tag="tp")
                 for h in range(2):
+                    g, j = units[h]
                     for u in range(2):
                         s = 2 * h + u
-                        nc.tensor.transpose(tp[:, s * P : (s + 1) * P], src[:, 2 * pr + h, g, u, :], ident[:])
-                wbank[(c, g, pr)] = tp
+                        nc.tensor.transpose(tp[:, s * P : (s + 1) * P], src[:, j, g, u, :], ident[:])
+                wbank[(c, units)] = tp
 
-        def e_w(c, order):
-            gwc = gwp.tile([P, G, 4, P, 4], BF16, name="gw", tag="gw", align_bytes=64)
-            gw[c] = gwc
-            for g, pr in order:
-                view = wbank[(c, g, pr)][:].bitcast(BF16)
+        def e_w(c, banks):
+            if c not in gw:
+                gwn = gwp.tile([P, G, 4, P, 4], BF16, name="gw", tag="gw", align_bytes=64)
+                gw[c] = gwn
+            gwc = gw[c]
+            for units in banks:
+                view = wbank[(c, units)][:].bitcast(BF16)
                 for h in range(2):
-                    j = 2 * pr + h
+                    g, j = units[h]
                     col = (4 * c + j) * 2 + g
                     nc.scalar.activation(
                         out=gwc[:, g, j, :, :].rearrange("p r (u e) -> p r u e", e=2),
@@ -148,7 +153,7 @@ def tile_fp8columnparallellinear_kernel(tc, x, weight, weight_scale_inv, bias, o
                     start=True,
                     stop=True,
                 )
-            nc.scalar.copy(out=bias_bc[q][:], in_=pb[:])
+            nc.vector.tensor_copy(out=bias_bc[q][:], in_=pb[:])
 
         acc = {}
         stage = {}
@@ -175,19 +180,25 @@ def tile_fp8columnparallellinear_kernel(tc, x, weight, weight_scale_inv, bias, o
                 st = stp.tile([P, 2, 512], F32, name="st", tag="st")
                 stage[(c, i)] = st
             b = bias_bc[c // 2][:, (c % 2) * 512 : (c % 2) * 512 + 512]
-            nc.vector.tensor_tensor(out=stage[(c, i)][:, t2, :], in0=acc[(c, t)][:], in1=b, op=ADD)
+            if 8 * c + t in ASSIST:
+                nc.scalar.copy(out=stage[(c, i)][:, t2, :], in_=acc[(c, t)][:])
+                nc.gpsimd.tensor_tensor(out=stage[(c, i)][:, t2, :], in0=stage[(c, i)][:, t2, :], in1=b, op=ADD)
+            else:
+                nc.vector.tensor_tensor(out=stage[(c, i)][:, t2, :], in0=acc[(c, t)][:], in1=b, op=ADD)
             cols = slice(c * 512, (c + 1) * 512)
             if c == NCH - 1 and i == NPIECE - 1:
                 nc.sync.dma_start(out=o_view[:, t, cols], in_=stage[(c, i)][:, t2, :])
             elif t2 == 1:
                 nc.sync.dma_start(out=o_view[:, 2 * i : 2 * i + 2, cols], in_=stage[(c, i)][:])
 
-        pair_major = [(0, 0), (1, 0), (0, 1), (1, 1)]
-        pass_major = [(0, 0), (0, 1), (1, 0), (1, 1)]
+        block_major = [((0, j), (1, j)) for j in range(4)]
+        pass_major = [((g, 2 * pr), (g, 2 * pr + 1)) for g in range(G) for pr in range(2)]
 
+        t_w(0, block_major[0:2])
+        e_w(0, block_major[0:2])
         b_cast(0)
-        t_w(0, pair_major)
-        e_w(0, pair_major)
+        t_w(0, block_major[2:4])
+        e_w(0, block_major[2:4])
         t_x(0)
         t_x(1)
         e_x(0, "v")

@@ -18,7 +18,6 @@ G = K // 512
 NCH = N // 512
 TB = M // P
 NPIECE = TB // 2
-ASSIST = (47, 50, 53, 56, 59)
 
 
 def tile_fp8columnparallellinear_kernel(tc, x, weight, weight_scale_inv, bias, out):
@@ -26,7 +25,7 @@ def tile_fp8columnparallellinear_kernel(tc, x, weight, weight_scale_inv, bias, o
     with ExitStack() as ctx:
         const = ctx.enter_context(tc.tile_pool(name="const", bufs=1))
         gwp = ctx.enter_context(tc.tile_pool(name="gwp", bufs=2))
-        stp = ctx.enter_context(tc.tile_pool(name="stp", bufs=6))
+        stp = ctx.enter_context(tc.tile_pool(name="stp", bufs=10))
         psum = ctx.enter_context(tc.psum_pool(name="psum", bufs=4))
         ctx.enter_context(tc.manual_schedule())
 
@@ -58,15 +57,20 @@ def tile_fp8columnparallellinear_kernel(tc, x, weight, weight_scale_inv, bias, o
                 nc.sync.dma_start(out=b_rows[0:NCH, :], in_=bias.rearrange("(c n) -> c n", c=NCH))
         for i in range(NPIECE):
             nc.sync.dma_start(out=x_sb[i][:], in_=x_view[:, 2 * i : 2 * i + 2, :])
-        load_w(1)
-        load_w(2)
-        load_w(3)
+        for c in range(1, NCH):
+            load_w(c)
 
-        s_nat = const.tile([P, 64], F32, name="s_nat")
+        s_nat = const.tile([P, 32], F32, name="s_nat")
         for q in range(4):
             nc.vector.tensor_copy(
-                out=s_nat[32 * q : 32 * q + 32, :].rearrange("p (j g) -> p j g", g=2),
-                in_=s_all[32 * q : 32 * q + 32, :].rearrange("p (j g q) -> p j g q", g=2, q=4)[:, :, :, q],
+                out=s_nat[32 * q : 32 * q + 32, :],
+                in_=s_all[32 * q : 32 * q + 32, :].rearrange("p (j g q) -> p j g q", g=2, q=4)[:, :, 0, q],
+            )
+        s_con = const.tile([P, 64], F32, name="s_con")
+        for hh in range(2):
+            nc.vector.tensor_copy(
+                out=s_con[64 * hh : 64 * hh + 64, :].rearrange("p (j u) -> p j u", u=2),
+                in_=s_all[64 * hh : 64 * hh + 64, :].rearrange("p (j g u h) -> p j g u h", g=2, u=2, h=2)[:, :, 1, :, hh],
             )
 
         xq = [const.tile([P, 512], U32, name="xq%d" % i, align_bytes=64) for i in range(NPIECE)]
@@ -78,18 +82,20 @@ def tile_fp8columnparallellinear_kernel(tc, x, weight, weight_scale_inv, bias, o
         wbank = {}
         xbank = {}
 
-        def words(tile_ap):
-            return tile_ap.bitcast(F32).rearrange("p j (g w u) -> p j g u w", g=G, u=2)
+        def words(tile_ap, j, g, u):
+            f = tile_ap.bitcast(F32)
+            if g == 0:
+                return f[:, j, 0:256].rearrange("p (w u) -> p u w", u=2)[:, u, :]
+            return f[:, j, 256 + P * u : 256 + P * u + P]
 
         def t_w(c, banks):
-            src = words(w_sb[c][:])
             for units in banks:
                 tp = psum.tile([P, 512], F32, name="tp", tag="tp")
                 for h in range(2):
                     g, j = units[h]
                     for u in range(2):
                         s = 2 * h + u
-                        nc.tensor.transpose(tp[:, s * P : (s + 1) * P], src[:, j, g, u, :], ident[:])
+                        nc.tensor.transpose(tp[:, s * P : (s + 1) * P], words(w_sb[c][:], j, g, u), ident[:])
                 wbank[(c, units)] = tp
 
         def e_w(c, banks):
@@ -101,13 +107,23 @@ def tile_fp8columnparallellinear_kernel(tc, x, weight, weight_scale_inv, bias, o
                 view = wbank[(c, units)][:].bitcast(BF16)
                 for h in range(2):
                     g, j = units[h]
-                    col = (4 * c + j) * 2 + g
-                    nc.scalar.activation(
-                        out=gwc[:, g, j, :, :].rearrange("p r (u e) -> p r u e", e=2),
-                        in_=view[:, h * 512 : (h + 1) * 512].rearrange("p (u r e) -> p r u e", u=2, e=2),
-                        func=COPY,
-                        scale=s_nat[:, col : col + 1],
-                    )
+                    jj = 4 * c + j
+                    if g == 0:
+                        nc.scalar.activation(
+                            out=gwc[:, g, j, :, :].rearrange("p r (u e) -> p r u e", e=2),
+                            in_=view[:, h * 512 : (h + 1) * 512].rearrange("p (u r e) -> p r u e", u=2, e=2),
+                            func=COPY,
+                            scale=s_nat[:, jj : jj + 1],
+                        )
+                    else:
+                        for u in range(2):
+                            lo = h * 512 + u * 256
+                            nc.scalar.activation(
+                                out=gwc[:, g, j, :, 2 * u : 2 * u + 2],
+                                in_=view[:, lo : lo + 256].rearrange("p (r e) -> p r e", e=2),
+                                func=COPY,
+                                scale=s_con[:, 2 * jj + u : 2 * jj + u + 1],
+                            )
 
         def q_w(c, g):
             nc.vector.quantize_mx(
@@ -117,13 +133,12 @@ def tile_fp8columnparallellinear_kernel(tc, x, weight, weight_scale_inv, bias, o
             )
 
         def t_x(i):
-            src = words(x_sb[i][:])
             for t2 in range(2):
                 tx = psum.tile([P, 512], F32, name="tx", tag="acc")
                 for g in range(G):
                     for u in range(2):
                         s = 2 * g + u
-                        nc.tensor.transpose(tx[:, s * P : (s + 1) * P], src[:, t2, g, u, :], ident[:])
+                        nc.tensor.transpose(tx[:, s * P : (s + 1) * P], words(x_sb[i][:], t2, g, u), ident[:])
                 xbank[(i, t2)] = tx
 
         def e_x(i, engine):
@@ -180,11 +195,7 @@ def tile_fp8columnparallellinear_kernel(tc, x, weight, weight_scale_inv, bias, o
                 st = stp.tile([P, 2, 512], F32, name="st", tag="st")
                 stage[(c, i)] = st
             b = bias_bc[c // 2][:, (c % 2) * 512 : (c % 2) * 512 + 512]
-            if 8 * c + t in ASSIST:
-                nc.scalar.copy(out=stage[(c, i)][:, t2, :], in_=acc[(c, t)][:])
-                nc.gpsimd.tensor_tensor(out=stage[(c, i)][:, t2, :], in0=stage[(c, i)][:, t2, :], in1=b, op=ADD)
-            else:
-                nc.vector.tensor_tensor(out=stage[(c, i)][:, t2, :], in0=acc[(c, t)][:], in1=b, op=ADD)
+            nc.vector.tensor_tensor(out=stage[(c, i)][:, t2, :], in0=acc[(c, t)][:], in1=b, op=ADD)
             cols = slice(c * 512, (c + 1) * 512)
             if c == NCH - 1 and i == NPIECE - 1:
                 nc.sync.dma_start(out=o_view[:, t, cols], in_=stage[(c, i)][:, t2, :])
@@ -216,7 +227,7 @@ def tile_fp8columnparallellinear_kernel(tc, x, weight, weight_scale_inv, bias, o
         t_w(1, pass_major)
         e_w(1, pass_major)
 
-        RUN = 6
+        RUN = 7
         for tau in range(NCH * TB):
             c, t = tau // TB, tau % TB
             if tau > 0 and tau % RUN == 0 and tau // RUN + 1 < NCH:
@@ -230,7 +241,5 @@ def tile_fp8columnparallellinear_kernel(tc, x, weight, weight_scale_inv, bias, o
                 base = RUN * (cn - 1)
                 if tau == base + 3:
                     q_w(cn, 0)
-                if tau == base + (5 if cn == 1 else 6):
+                if tau == base + (6 if cn == 1 else 7):
                     q_w(cn, 1)
-            if tau % RUN == 1 and tau // RUN + 4 < NCH:
-                load_w(tau // RUN + 4)

@@ -24,8 +24,9 @@ def tile_fp8columnparallellinear_kernel(tc, x, weight, weight_scale_inv, bias, o
     nc = tc.nc
     with ExitStack() as ctx:
         const = ctx.enter_context(tc.tile_pool(name="const", bufs=1))
+        wp = ctx.enter_context(tc.tile_pool(name="wp", bufs=5))
         gwp = ctx.enter_context(tc.tile_pool(name="gwp", bufs=2))
-        stp = ctx.enter_context(tc.tile_pool(name="stp", bufs=10))
+        stp = ctx.enter_context(tc.tile_pool(name="stp", bufs=9))
         psum = ctx.enter_context(tc.psum_pool(name="psum", bufs=4))
         ctx.enter_context(tc.manual_schedule())
 
@@ -44,21 +45,30 @@ def tile_fp8columnparallellinear_kernel(tc, x, weight, weight_scale_inv, bias, o
         ident = const.tile([P, P], F32, name="ident")
         make_identity(nc, ident[:])
 
-        w_sb = [const.tile([P, 4, K], BF16, name="w_sb%d" % c) for c in range(NCH)]
+        w_sb = {}
         x_sb = [const.tile([P, 2, K], BF16, name="x_sb%d" % i) for i in range(NPIECE)]
         bias_bc = [const.tile([P, 1024], BF16, name="bias_bc%d" % q) for q in range(4)]
 
-        def load_w(c):
-            nc.sync.dma_start(out=w_sb[c][:], in_=w_view[:, 4 * c : 4 * c + 4, :])
+        def load_w(c, pieces):
+            wt = wp.tile([P, 4, K], BF16, name="w_sb", tag="w_sb")
+            w_sb[c] = wt
+            step = 4 // pieces
+            for a in range(pieces):
+                nc.sync.dma_start(
+                    out=wt[:, a * step : (a + 1) * step, :],
+                    in_=w_view[:, 4 * c + a * step : 4 * c + (a + 1) * step, :],
+                )
+                if c == 0 and a == 0:
+                    nc.sync.dma_start(out=b_rows[0:NCH, :], in_=bias.rearrange("(c n) -> c n", c=NCH))
 
-        for j in range(4):
-            nc.sync.dma_start(out=w_sb[0][:, j, :], in_=w_view[:, j, :])
-            if j == 0:
-                nc.sync.dma_start(out=b_rows[0:NCH, :], in_=bias.rearrange("(c n) -> c n", c=NCH))
-        for i in range(NPIECE):
+        def load_x(i):
             nc.sync.dma_start(out=x_sb[i][:], in_=x_view[:, 2 * i : 2 * i + 2, :])
+
+        load_w(0, 4)
+        for i in range(NPIECE):
+            load_x(i)
         for c in range(1, NCH):
-            load_w(c)
+            load_w(c, 1)
 
         s_nat = const.tile([P, 32], F32, name="s_nat")
         for q in range(4):
@@ -191,16 +201,21 @@ def tile_fp8columnparallellinear_kernel(tc, x, weight, weight_scale_inv, bias, o
 
         def o(c, t):
             i, t2 = t // 2, t % 2
-            if t2 == 0:
-                st = stp.tile([P, 2, 512], F32, name="st", tag="st")
-                stage[(c, i)] = st
-            b = bias_bc[c // 2][:, (c % 2) * 512 : (c % 2) * 512 + 512]
-            nc.vector.tensor_tensor(out=stage[(c, i)][:, t2, :], in0=acc[(c, t)][:], in1=b, op=ADD)
-            cols = slice(c * 512, (c + 1) * 512)
-            if c == NCH - 1 and i == NPIECE - 1:
-                nc.sync.dma_start(out=o_view[:, t, cols], in_=stage[(c, i)][:, t2, :])
+            s, half = c // 2, c % 2
+            if t2 == 0 and half == 0:
+                st = stp.tile([P, 2, 1024], F32, name="st", tag="st")
+                stage[(s, i)] = st
+            st = stage[(s, i)]
+            here = slice(half * 512, half * 512 + 512)
+            nc.vector.tensor_tensor(out=st[:, t2, here], in0=acc[(c, t)][:], in1=bias_bc[s][:, here], op=ADD)
+            rows = slice(2 * i, 2 * i + 2)
+            if s < 2:
+                if half == 1 and t2 == 1:
+                    nc.sync.dma_start(out=o_view[:, rows, s * 1024 : (s + 1) * 1024], in_=st[:])
+            elif c == NCH - 1 and i == NPIECE - 1:
+                nc.sync.dma_start(out=o_view[:, t, c * 512 : (c + 1) * 512], in_=st[:, t2, here])
             elif t2 == 1:
-                nc.sync.dma_start(out=o_view[:, 2 * i : 2 * i + 2, cols], in_=stage[(c, i)][:])
+                nc.sync.dma_start(out=o_view[:, rows, c * 512 : (c + 1) * 512], in_=st[:, :, here])
 
         block_major = [((0, j), (1, j)) for j in range(4)]
         pass_major = [((g, 2 * pr), (g, 2 * pr + 1)) for g in range(G) for pr in range(2)]

@@ -178,7 +178,10 @@ def tile_fp8columnparallellinear_kernel(tc, x, weight, weight_scale_inv, bias, o
                     start=True,
                     stop=True,
                 )
-            nc.vector.tensor_copy(out=bias_bc[q][:], in_=pb[:])
+            if q == 0:
+                nc.vector.tensor_copy(out=bias_bc[q][:], in_=pb[:])
+            else:
+                nc.scalar.copy(out=bias_bc[q][:], in_=pb[:])
 
         acc = {}
         stage = {}

@@ -178,10 +178,7 @@ def tile_fp8columnparallellinear_kernel(tc, x, weight, weight_scale_inv, bias, o
                     start=True,
                     stop=True,
                 )
-            if q == 0:
-                nc.vector.tensor_copy(out=bias_bc[q][:], in_=pb[:])
-            else:
-                nc.scalar.copy(out=bias_bc[q][:], in_=pb[:])
+            nc.vector.tensor_copy(out=bias_bc[q][:], in_=pb[:])
 
         acc = {}
         stage = {}
@@ -248,16 +245,25 @@ def tile_fp8columnparallellinear_kernel(tc, x, weight, weight_scale_inv, bias, o
         RUN = 7
         for tau in range(NCH * TB):
             c, t = tau // TB, tau % TB
-            if tau > 0 and tau % RUN == 0 and tau // RUN + 1 < NCH:
-                if tau // RUN < 4:
-                    b_cast(tau // RUN)
-                t_w(tau // RUN + 1, pass_major)
-                e_w(tau // RUN + 1, pass_major)
+            for cn in range(2, NCH):
+                base = RUN * (cn - 1)
+                if tau == base:
+                    if cn - 1 < 4:
+                        b_cast(cn - 1)
+                    t_w(cn, pass_major[0:2])
+                    e_w(cn, pass_major[0:2])
+                if tau == base + 3:
+                    t_w(cn, pass_major[2:4])
+                    e_w(cn, pass_major[2:4])
             mx(c, t)
             o(c, t)
-            for cn in range(1, NCH):
+            if tau == 3:
+                q_w(1, 0)
+            if tau == 6:
+                q_w(1, 1)
+            for cn in range(2, NCH):
                 base = RUN * (cn - 1)
-                if tau == base + 3:
+                if tau == base + 4:
                     q_w(cn, 0)
-                if tau == base + (6 if cn == 1 else 7):
+                if tau == min(base + 9, TB * cn - 3):
                     q_w(cn, 1)

@@ -10,6 +10,7 @@ U8 = mybir.dt.uint8
 FP8X4 = mybir.dt.float8_e4m3fn_x4
 COPY = mybir.ActivationFunctionType.Copy
 ADD = mybir.AluOpType.add
+MULT = mybir.AluOpType.mult
 
 P = 128
 M, K, N = 1024, 1024, 4096
@@ -36,10 +37,13 @@ def tile_fp8columnparallellinear_kernel(tc, x, weight, weight_scale_inv, bias, o
 
         b_rows = const.tile([P, 512], BF16, name="b_rows")
         nc.vector.memset(b_rows[:], 0.0)
-        s_all = const.tile([P, 256], BF16, name="s_all")
         nc.scalar.dma_start(
-            out=s_all[:], in_=weight_scale_inv.rearrange("a b -> (a b)").partition_broadcast(P)
+            out=b_rows[NCH : NCH + 1, 0:256], in_=weight_scale_inv.rearrange("(o a) b -> o (a b)", o=1)
         )
+        first_in = const.tile([P, 1], F32, name="first_in")
+        nc.gpsimd.memset(first_in[:], 0.0)
+        first_act = const.tile([P, 1], F32, name="first_act")
+        nc.scalar.activation(out=first_act[:], in_=first_in[:], func=COPY, scale=1.0)
         ident_bf = const.tile([P, P], BF16, name="ident_bf")
         make_identity(nc, ident_bf[:])
         ident = const.tile([P, P], F32, name="ident")
@@ -70,6 +74,14 @@ def tile_fp8columnparallellinear_kernel(tc, x, weight, weight_scale_inv, bias, o
         for c in range(1, NCH):
             load_w(c, 1)
 
+        s_all = psum.tile([P, 256], F32, name="s_all", tag="acc")
+        nc.tensor.matmul(
+            out=s_all[:],
+            lhsT=ident_bf[:, NCH : NCH + 1].to_broadcast([P, P]),
+            rhs=b_rows[:, 0:256],
+            start=True,
+            stop=True,
+        )
         s_nat = const.tile([P, 32], F32, name="s_nat")
         for q in range(4):
             nc.vector.tensor_copy(
@@ -108,31 +120,38 @@ def tile_fp8columnparallellinear_kernel(tc, x, weight, weight_scale_inv, bias, o
                         nc.tensor.transpose(tp[:, s * P : (s + 1) * P], words(w_sb[c][:], j, g, u), ident[:])
                 wbank[(c, units)] = tp
 
-        def e_w(c, banks):
+        def scaled_copy(engine, dst, src, scale):
+            if engine == "s":
+                nc.scalar.activation(out=dst, in_=src, func=COPY, scale=scale)
+            else:
+                nc.vector.tensor_scalar(out=dst, in0=src, scalar1=scale, scalar2=None, op0=MULT)
+
+        def e_w(c, banks, engines):
             if c not in gw:
                 gwn = gwp.tile([P, G, 4, P, 4], BF16, name="gw", tag="gw", align_bytes=64)
                 gw[c] = gwn
             gwc = gw[c]
-            for units in banks:
+            for b, units in enumerate(banks):
+                engine = engines[b]
                 view = wbank[(c, units)][:].bitcast(BF16)
                 for h in range(2):
                     g, j = units[h]
                     jj = 4 * c + j
                     if g == 0:
-                        nc.scalar.activation(
-                            out=gwc[:, g, j, :, :].rearrange("p r (u e) -> p r u e", e=2),
-                            in_=view[:, h * 512 : (h + 1) * 512].rearrange("p (u r e) -> p r u e", u=2, e=2),
-                            func=COPY,
-                            scale=s_nat[:, jj : jj + 1],
+                        scaled_copy(
+                            engine,
+                            gwc[:, g, j, :, :].rearrange("p r (u e) -> p r u e", e=2),
+                            view[:, h * 512 : (h + 1) * 512].rearrange("p (u r e) -> p r u e", u=2, e=2),
+                            s_nat[:, jj : jj + 1],
                         )
                     else:
                         for u in range(2):
                             lo = h * 512 + u * 256
-                            nc.scalar.activation(
-                                out=gwc[:, g, j, :, 2 * u : 2 * u + 2],
-                                in_=view[:, lo : lo + 256].rearrange("p (r e) -> p r e", e=2),
-                                func=COPY,
-                                scale=s_con[:, 2 * jj + u : 2 * jj + u + 1],
+                            scaled_copy(
+                                engine,
+                                gwc[:, g, j, :, 2 * u : 2 * u + 2],
+                                view[:, lo : lo + 256].rearrange("p (r e) -> p r e", e=2),
+                                s_con[:, 2 * jj + u : 2 * jj + u + 1],
                             )
 
         def q_w(c, g):
@@ -151,9 +170,10 @@ def tile_fp8columnparallellinear_kernel(tc, x, weight, weight_scale_inv, bias, o
                         nc.tensor.transpose(tx[:, s * P : (s + 1) * P], words(x_sb[i][:], t2, g, u), ident[:])
                 xbank[(i, t2)] = tx
 
-        def e_x(i, engine):
+        def e_x(i, engines):
             dst = gx[i][:].bitcast(F32)
             for t2 in range(2):
+                engine = engines[t2]
                 src = xbank[(i, t2)][:].rearrange("p (g u r) -> p g r u", g=G, u=2)
                 if engine == "v":
                     nc.vector.tensor_copy(out=dst[:, :, t2, :, :], in_=src)
@@ -220,27 +240,25 @@ def tile_fp8columnparallellinear_kernel(tc, x, weight, weight_scale_inv, bias, o
         block_major = [((0, j), (1, j)) for j in range(4)]
         pass_major = [((g, 2 * pr), (g, 2 * pr + 1)) for g in range(G) for pr in range(2)]
 
-        t_w(0, block_major[0:2])
-        e_w(0, block_major[0:2])
-        b_cast(0)
-        t_w(0, block_major[2:4])
-        e_w(0, block_major[2:4])
+        t_w(0, block_major)
+        e_w(0, block_major, "svsv")
         t_x(0)
         t_x(1)
-        e_x(0, "v")
-        e_x(1, "v")
-        t_x(2)
-        t_x(3)
-        e_x(2, "s")
-        e_x(3, "s")
+        e_x(0, "vs")
         q_w(0, 0)
+        e_x(1, "vs")
         q_x(0)
         q_w(0, 1)
+        t_x(2)
+        t_x(3)
+        e_x(2, "sv")
         q_x(1)
+        e_x(3, "sv")
         q_x(2)
+        b_cast(0)
         q_x(3)
         t_w(1, pass_major)
-        e_w(1, pass_major)
+        e_w(1, pass_major, "ssss")
 
         RUN = 7
         for tau in range(NCH * TB):
@@ -251,10 +269,10 @@ def tile_fp8columnparallellinear_kernel(tc, x, weight, weight_scale_inv, bias, o
                     if cn - 1 < 4:
                         b_cast(cn - 1)
                     t_w(cn, pass_major[0:2])
-                    e_w(cn, pass_major[0:2])
+                    e_w(cn, pass_major[0:2], "ss")
                 if tau == base + 3:
                     t_w(cn, pass_major[2:4])
-                    e_w(cn, pass_major[2:4])
+                    e_w(cn, pass_major[2:4], "ss")
             mx(c, t)
             o(c, t)
             if tau == 3:

@@ -95,11 +95,11 @@ def tile_fp8columnparallellinear_kernel(tc, x, weight, weight_scale_inv, bias, o
                 in_=s_all[64 * hh : 64 * hh + 64, :].rearrange("p (j g u h) -> p j g u h", g=2, u=2, h=2)[:, :, 1, :, hh],
             )
 
-        xq = [const.tile([P, 512], U32, name="xq%d" % i, align_bytes=64) for i in range(NPIECE)]
-        xs = [const.tile([P, 512], U8, name="xs%d" % i, align_bytes=64) for i in range(NPIECE)]
+        xq = [const.tile([P, 512], U32, name="xq%d" % i, align_bytes=256) for i in range(NPIECE)]
+        xs = [const.tile([P, 512], U8, name="xs%d" % i, align_bytes=256) for i in range(NPIECE)]
         gx = [const.tile([P, 2, 2, P, 4], BF16, name="gx%d" % i, align_bytes=64) for i in range(NPIECE)]
-        wq = [const.tile([P, G, 512], U32, name="wq%d" % c, align_bytes=64) for c in range(NCH)]
-        ws = [const.tile([P, G, 512], U8, name="ws%d" % c, align_bytes=64) for c in range(NCH)]
+        wq = [const.tile([P, G, 512], U32, name="wq%d" % c, align_bytes=256) for c in range(NCH)]
+        ws = [const.tile([P, G, 512], U8, name="ws%d" % c, align_bytes=256) for c in range(NCH)]
         gw = {}
         wbank = {}
         xbank = {}

@@ -82,18 +82,14 @@ def tile_fp8columnparallellinear_kernel(tc, x, weight, weight_scale_inv, bias, o
             start=True,
             stop=True,
         )
-        s_nat = const.tile([P, 32], F32, name="s_nat")
-        for q in range(4):
-            nc.vector.tensor_copy(
-                out=s_nat[32 * q : 32 * q + 32, :],
-                in_=s_all[32 * q : 32 * q + 32, :].rearrange("p (j g q) -> p j g q", g=2, q=4)[:, :, 0, q],
-            )
-        s_con = const.tile([P, 64], F32, name="s_con")
+        s_con = const.tile([P, 32, G, 2], F32, name="s_con")
+        s_four = const.tile([P, 32, G, 2, 2], BF16, name="s_four")
         for hh in range(2):
-            nc.vector.tensor_copy(
-                out=s_con[64 * hh : 64 * hh + 64, :].rearrange("p (j u) -> p j u", u=2),
-                in_=s_all[64 * hh : 64 * hh + 64, :].rearrange("p (j g u h) -> p j g u h", g=2, u=2, h=2)[:, :, 1, :, hh],
-            )
+            part = slice(64 * hh, 64 * hh + 64)
+            src = s_all[part, :].rearrange("p (j g u h) -> p j g u h", g=G, u=2, h=2)[:, :, :, :, hh]
+            nc.vector.tensor_copy(out=s_con[part, :, :, :], in_=src)
+        for e in range(2):
+            nc.vector.tensor_copy(out=s_four[:, :, :, :, e], in_=s_con[:])
 
         xq = [const.tile([P, 512], U32, name="xq%d" % i, align_bytes=256) for i in range(NPIECE)]
         xs = [const.tile([P, 512], U8, name="xs%d" % i, align_bytes=256) for i in range(NPIECE)]
@@ -105,10 +101,8 @@ def tile_fp8columnparallellinear_kernel(tc, x, weight, weight_scale_inv, bias, o
         xbank = {}
 
         def words(tile_ap, j, g, u):
-            f = tile_ap.bitcast(F32)
-            if g == 0:
-                return f[:, j, 0:256].rearrange("p (w u) -> p u w", u=2)[:, u, :]
-            return f[:, j, 256 + P * u : 256 + P * u + P]
+            lo = 256 * g + P * u
+            return tile_ap.bitcast(F32)[:, j, lo : lo + P]
 
         def t_w(c, banks):
             for units in banks:
@@ -120,38 +114,31 @@ def tile_fp8columnparallellinear_kernel(tc, x, weight, weight_scale_inv, bias, o
                         nc.tensor.transpose(tp[:, s * P : (s + 1) * P], words(w_sb[c][:], j, g, u), ident[:])
                 wbank[(c, units)] = tp
 
-        def scaled_copy(engine, dst, src, scale):
-            if engine == "s":
-                nc.scalar.activation(out=dst, in_=src, func=COPY, scale=scale)
-            else:
-                nc.vector.tensor_scalar(out=dst, in0=src, scalar1=scale, scalar2=None, op0=MULT)
-
         def e_w(c, banks, engines):
             if c not in gw:
                 gwn = gwp.tile([P, G, 4, P, 4], BF16, name="gw", tag="gw", align_bytes=64)
                 gw[c] = gwn
             gwc = gw[c]
             for b, units in enumerate(banks):
-                engine = engines[b]
                 view = wbank[(c, units)][:].bitcast(BF16)
                 for h in range(2):
                     g, j = units[h]
                     jj = 4 * c + j
-                    if g == 0:
-                        scaled_copy(
-                            engine,
-                            gwc[:, g, j, :, :].rearrange("p r (u e) -> p r u e", e=2),
-                            view[:, h * 512 : (h + 1) * 512].rearrange("p (u r e) -> p r u e", u=2, e=2),
-                            s_nat[:, jj : jj + 1],
+                    if engines[b] == "v":
+                        nc.vector.tensor_tensor(
+                            out=gwc[:, g, j, :, :].rearrange("p r (u e) -> p r u e", e=2),
+                            in0=view[:, h * 512 : (h + 1) * 512].rearrange("p (u r e) -> p r u e", u=2, e=2),
+                            in1=s_four[:, jj, g, :, :].unsqueeze(1).to_broadcast([P, P, 2, 2]),
+                            op=MULT,
                         )
                     else:
                         for u in range(2):
                             lo = h * 512 + u * 256
-                            scaled_copy(
-                                engine,
-                                gwc[:, g, j, :, 2 * u : 2 * u + 2],
-                                view[:, lo : lo + 256].rearrange("p (r e) -> p r e", e=2),
-                                s_con[:, 2 * jj + u : 2 * jj + u + 1],
+                            nc.scalar.activation(
+                                out=gwc[:, g, j, :, 2 * u : 2 * u + 2],
+                                in_=view[:, lo : lo + 256].rearrange("p (r e) -> p r e", e=2),
+                                func=COPY,
+                                scale=s_con[:, jj, g, u : u + 1],
                             )
 
         def q_w(c, g):
@@ -198,7 +185,7 @@ def tile_fp8columnparallellinear_kernel(tc, x, weight, weight_scale_inv, bias, o
                     start=True,
                     stop=True,
                 )
-            nc.vector.tensor_copy(out=bias_bc[q][:], in_=pb[:])
+            nc.scalar.copy(out=bias_bc[q][:], in_=pb[:])
 
         acc = {}
         stage = {}
@@ -241,24 +228,24 @@ def tile_fp8columnparallellinear_kernel(tc, x, weight, weight_scale_inv, bias, o
         pass_major = [((g, 2 * pr), (g, 2 * pr + 1)) for g in range(G) for pr in range(2)]
 
         t_w(0, block_major)
-        e_w(0, block_major, "svsv")
+        e_w(0, block_major, "vvvv")
         t_x(0)
         t_x(1)
-        e_x(0, "vs")
+        e_x(0, "ss")
         q_w(0, 0)
-        e_x(1, "vs")
+        e_x(1, "ss")
         q_x(0)
         q_w(0, 1)
         t_x(2)
         t_x(3)
-        e_x(2, "sv")
+        e_x(2, "ss")
         q_x(1)
-        e_x(3, "sv")
+        e_x(3, "ss")
         q_x(2)
         b_cast(0)
         q_x(3)
         t_w(1, pass_major)
-        e_w(1, pass_major, "ssss")
+        e_w(1, pass_major, "svsv")
 
         RUN = 7
         for tau in range(NCH * TB):
@@ -269,7 +256,7 @@ def tile_fp8columnparallellinear_kernel(tc, x, weight, weight_scale_inv, bias, o
                     if cn - 1 < 4:
                         b_cast(cn - 1)
                     t_w(cn, pass_major[0:2])
-                    e_w(cn, pass_major[0:2], "ss")
+                    e_w(cn, pass_major[0:2], "sv")
                 if tau == base + 3:
                     t_w(cn, pass_major[2:4])
                     e_w(cn, pass_major[2:4], "ss")

from contextlib import ExitStack

import concourse.mybir as mybir
from concourse.masks import make_identity

F32 = mybir.dt.float32
BF16 = mybir.dt.bfloat16
U32 = mybir.dt.uint32
U8 = mybir.dt.uint8
FP8X4 = mybir.dt.float8_e4m3fn_x4
COPY = mybir.ActivationFunctionType.Copy
ADD = mybir.AluOpType.add
MULT = mybir.AluOpType.mult

P = 128
M, K, N = 1024, 1024, 4096
FLOPS = 2 * M * K * N
G = K // 512
NCH = N // 512
TB = M // P
NPIECE = TB // 2


def tile_fp8columnparallellinear_kernel(tc, x, weight, weight_scale_inv, bias, out):
    nc = tc.nc
    with ExitStack() as ctx:
        const = ctx.enter_context(tc.tile_pool(name="const", bufs=1))
        wp = ctx.enter_context(tc.tile_pool(name="wp", bufs=5))
        gwp = ctx.enter_context(tc.tile_pool(name="gwp", bufs=2))
        stp = ctx.enter_context(tc.tile_pool(name="stp", bufs=9))
        psum = ctx.enter_context(tc.psum_pool(name="psum", bufs=4))
        ctx.enter_context(tc.manual_schedule())

        x_view = x.rearrange("(p t) k -> p t k", t=TB)
        w_view = weight.rearrange("(j p) k -> p j k", p=P)
        o_view = out.rearrange("(p t) n -> p t n", t=TB)

        b_rows = const.tile([P, 512], BF16, name="b_rows")
        nc.vector.memset(b_rows[:], 0.0)
        nc.scalar.dma_start(
            out=b_rows[NCH : NCH + 1, 0:256], in_=weight_scale_inv.rearrange("(o a) b -> o (a b)", o=1)
        )
        first_in = const.tile([P, 1], F32, name="first_in")
        nc.gpsimd.memset(first_in[:], 0.0)
        first_act = const.tile([P, 1], F32, name="first_act")
        nc.scalar.activation(out=first_act[:], in_=first_in[:], func=COPY, scale=1.0)
        ident_bf = const.tile([P, P], BF16, name="ident_bf")
        make_identity(nc, ident_bf[:])
        ident = const.tile([P, P], F32, name="ident")
        make_identity(nc, ident[:])

        w_sb = {}
        x_sb = [const.tile([P, 2, K], BF16, name="x_sb%d" % i) for i in range(NPIECE)]
        bias_bc = [const.tile([P, 1024], BF16, name="bias_bc%d" % q) for q in range(4)]

        def load_w(c, pieces):
            wt = wp.tile([P, 4, K], BF16, name="w_sb", tag="w_sb")
            w_sb[c] = wt
            step = 4 // pieces
            for a in range(pieces):
                nc.sync.dma_start(
                    out=wt[:, a * step : (a + 1) * step, :],
                    in_=w_view[:, 4 * c + a * step : 4 * c + (a + 1) * step, :],
                )
                if c == 0 and a == 0:
                    nc.sync.dma_start(out=b_rows[0:NCH, :], in_=bias.rearrange("(c n) -> c n", c=NCH))

        def load_x(i):
            nc.sync.dma_start(out=x_sb[i][:], in_=x_view[:, 2 * i : 2 * i + 2, :])

        load_w(0, 4)
        for i in range(NPIECE):
            load_x(i)
        for c in range(1, NCH):
            load_w(c, 1)

        s_all = psum.tile([P, 256], F32, name="s_all", tag="acc")
        nc.tensor.matmul(
            out=s_all[:],
            lhsT=ident_bf[:, NCH : NCH + 1].to_broadcast([P, P]),
            rhs=b_rows[:, 0:256],
            start=True,
            stop=True,
        )
        s_con = const.tile([P, 32, G, 2], F32, name="s_con")
        s_four = const.tile([P, 32, G, 2, 2], BF16, name="s_four")
        for hh in range(2):
            part = slice(64 * hh, 64 * hh + 64)
            src = s_all[part, :].rearrange("p (j g u h) -> p j g u h", g=G, u=2, h=2)[:, :, :, :, hh]
            nc.vector.tensor_copy(out=s_con[part, :, :, :], in_=src)
        for e in range(2):
            nc.vector.tensor_copy(out=s_four[:, :, :, :, e], in_=s_con[:])

        xq = [const.tile([P, 512], U32, name="xq%d" % i, align_bytes=256) for i in range(NPIECE)]
        xs = [const.tile([P, 512], U8, name="xs%d" % i, align_bytes=256) for i in range(NPIECE)]
        gx = [const.tile([P, 2, 2, P, 4], BF16, name="gx%d" % i, align_bytes=64) for i in range(NPIECE)]
        wq = [const.tile([P, G, 512], U32, name="wq%d" % c, align_bytes=256) for c in range(NCH)]
        ws = [const.tile([P, G, 512], U8, name="ws%d" % c, align_bytes=256) for c in range(NCH)]
        gw = {}
        wbank = {}
        xbank = {}

        def words(tile_ap, j, g, u):
            lo = 256 * g + P * u
            return tile_ap.bitcast(F32)[:, j, lo : lo + P]

        def t_w(c, banks):
            for units in banks:
                tp = psum.tile([P, 512], F32, name="tp", tag="tp")
                for h in range(2):
                    g, j = units[h]
                    for u in range(2):
                        s = 2 * h + u
                        nc.tensor.transpose(tp[:, s * P : (s + 1) * P], words(w_sb[c][:], j, g, u), ident[:])
                wbank[(c, units)] = tp

        def e_w(c, banks, engines):
            if c not in gw:
                gwn = gwp.tile([P, G, 4, P, 4], BF16, name="gw", tag="gw", align_bytes=64)
                gw[c] = gwn
            gwc = gw[c]
            for b, units in enumerate(banks):
                view = wbank[(c, units)][:].bitcast(BF16)
                for h in range(2):
                    g, j = units[h]
                    jj = 4 * c + j
                    if engines[b] == "v":
                        nc.vector.tensor_tensor(
                            out=gwc[:, g, j, :, :].rearrange("p r (u e) -> p r u e", e=2),
                            in0=view[:, h * 512 : (h + 1) * 512].rearrange("p (u r e) -> p r u e", u=2, e=2),
                            in1=s_four[:, jj, g, :, :].unsqueeze(1).to_broadcast([P, P, 2, 2]),
                            op=MULT,
                        )
                    else:
                        for u in range(2):
                            lo = h * 512 + u * 256
                            nc.scalar.activation(
                                out=gwc[:, g, j, :, 2 * u : 2 * u + 2],
                                in_=view[:, lo : lo + 256].rearrange("p (r e) -> p r e", e=2),
                                func=COPY,
                                scale=s_con[:, jj, g, u : u + 1],
                            )

        def q_w(c, g):
            nc.vector.quantize_mx(
                out=wq[c][:, g, :].bitcast(FP8X4),
                scales=ws[c][:, g, :],
                in_=gw[c][:, g, :, :, :].rearrange("p j r t -> p (j r t)"),
            )

        def t_x(i):
            for t2 in range(2):
                tx = psum.tile([P, 512], F32, name="tx", tag="acc")
                for g in range(G):
                    for u in range(2):
                        s = 2 * g + u
                        nc.tensor.transpose(tx[:, s * P : (s + 1) * P], words(x_sb[i][:], t2, g, u), ident[:])
                xbank[(i, t2)] = tx

        def e_x(i, engines):
            dst = gx[i][:].bitcast(F32)
            for t2 in range(2):
                engine = engines[t2]
                src = xbank[(i, t2)][:].rearrange("p (g u r) -> p g r u", g=G, u=2)
                if engine == "v":
                    nc.vector.tensor_copy(out=dst[:, :, t2, :, :], in_=src)
                else:
                    nc.scalar.copy(out=dst[:, :, t2, :, :], in_=src)

        def q_x(i):
            nc.vector.quantize_mx(
                out=xq[i][:].bitcast(FP8X4),
                scales=xs[i][:],
                in_=gx[i][:].rearrange("p g t r v -> p (g t r v)"),
            )

        def b_cast(q):
            pb = psum.tile([P, 1024], BF16, name="pb", tag="acc")
            for h in range(2):
                c = 2 * q + h
                nc.tensor.matmul(
                    out=pb[:, h * 512 : (h + 1) * 512],
                    lhsT=ident_bf[:, c : c + 1].to_broadcast([P, P]),
                    rhs=b_rows[:],
                    start=True,
                    stop=True,
                )
            nc.scalar.copy(out=bias_bc[q][:], in_=pb[:])

        acc = {}
        stage = {}

        def mx(c, t):
            i, t2 = t // 2, t % 2
            a = psum.tile([P, 512], F32, name="acc", tag="acc")
            acc[(c, t)] = a
            for g in range(G):
                cols = slice(g * 256 + t2 * P, g * 256 + t2 * P + P)
                nc.tensor.matmul_mx(
                    out=a[:],
                    lhsT=xq[i][:, cols].bitcast(FP8X4),
                    lhsT_scale=xs[i][:, cols],
                    rhs=wq[c][:, g, :].bitcast(FP8X4),
                    rhs_scale=ws[c][:, g, :],
                    start=(g == 0),
                    stop=(g == G - 1),
                )

        def o(c, t):
            i, t2 = t // 2, t % 2
            s, half = c // 2, c % 2
            if t2 == 0 and half == 0:
                st = stp.tile([P, 2, 1024], F32, name="st", tag="st")
                stage[(s, i)] = st
            st = stage[(s, i)]
            here = slice(half * 512, half * 512 + 512)
            nc.vector.tensor_tensor(out=st[:, t2, here], in0=acc[(c, t)][:], in1=bias_bc[s][:, here], op=ADD)
            rows = slice(2 * i, 2 * i + 2)
            if s < 2:
                if half == 1 and t2 == 1:
                    nc.sync.dma_start(out=o_view[:, rows, s * 1024 : (s + 1) * 1024], in_=st[:])
            elif c == NCH - 1 and i == NPIECE - 1:
                nc.sync.dma_start(out=o_view[:, t, c * 512 : (c + 1) * 512], in_=st[:, t2, here])
            elif t2 == 1:
                nc.sync.dma_start(out=o_view[:, rows, c * 512 : (c + 1) * 512], in_=st[:, :, here])

        block_major = [((0, j), (1, j)) for j in range(4)]
        pass_major = [((g, 2 * pr), (g, 2 * pr + 1)) for g in range(G) for pr in range(2)]

        t_w(0, block_major)
        e_w(0, block_major, "vvvv")
        t_x(0)
        t_x(1)
        e_x(0, "ss")
        q_w(0, 0)
        e_x(1, "ss")
        q_x(0)
        q_w(0, 1)
        t_x(2)
        t_x(3)
        e_x(2, "ss")
        q_x(1)
        e_x(3, "ss")
        q_x(2)
        b_cast(0)
        q_x(3)
        t_w(1, pass_major)
        e_w(1, pass_major, "svsv")

        RUN = 7
        for tau in range(NCH * TB):
            c, t = tau // TB, tau % TB
            for cn in range(2, NCH):
                base = RUN * (cn - 1)
                if tau == base:
                    if cn - 1 < 4:
                        b_cast(cn - 1)
                    t_w(cn, pass_major[0:2])
                    e_w(cn, pass_major[0:2], "sv")
                if tau == base + 3:
                    t_w(cn, pass_major[2:4])
                    e_w(cn, pass_major[2:4], "ss")
            mx(c, t)
            o(c, t)
            if tau == 3:
                q_w(1, 0)
            if tau == 6:
                q_w(1, 1)
            for cn in range(2, NCH):
                base = RUN * (cn - 1)
                if tau == base + 4:
                    q_w(cn, 0)
                if tau == min(base + 9, TB * cn - 3):
                    q_w(cn, 1)
